import numpy as np
import ml_dtypes


def mxq(x, axis, fmt="e4m3"):
    dtype, down = {"e4m3": (ml_dtypes.float8_e4m3fn, 7), "e5m2": (ml_dtypes.float8_e5m2, 14)}[fmt]
    v = np.moveaxis(np.asarray(x, np.float32).astype(ml_dtypes.bfloat16).astype(np.float64), axis, -1)
    blocks = v.reshape(v.shape[:-1] + (-1, 32))
    amax = np.abs(blocks).max(-1, keepdims=True)
    byte = np.maximum(np.where(amax > 0, np.frexp(amax)[1] - 1 + 127, 0) - down, 1)
    scale = np.exp2(byte - 127.0)
    codes = (blocks / scale).astype(np.float32).astype(dtype).astype(np.float64)
    return np.moveaxis((codes * scale).reshape(v.shape), -1, axis)


WIDE = False


def mx_kscale(k):
    if not WIDE:
        return np.ones(k)
    levels = np.array([10, -10, 5, -5, 0])
    a = np.random.permutation(np.resize(levels, k // 512 * 4)).reshape(k // 512, 4)
    idx = np.arange(k)
    return np.exp2(a[idx // 512, idx % 128 // 32])


BF16 = ml_dtypes.bfloat16


def bf(x):
    return np.asarray(x, np.float32).astype(BF16)


def f64(x):
    return np.asarray(x).astype(np.float64)


B, H, S, D = 1, 16, 1024, 128
G = 1.3
A = np.sqrt(np.log(S) * np.sqrt(D) / (D - 1))
Q0 = np.log(2.0) * np.sqrt(D)


def restricted_softmax(src, margin=0.0):
    src_max = np.maximum(np.max(src, axis=-1, keepdims=True), 0.0)
    out = np.exp(src - src_max)
    denom = np.sum(out, axis=-1, keepdims=True) + np.exp(margin - src_max)
    return out / denom


def setup_inputs():
    s = mx_kscale(S)
    t = s / s.max()
    q = np.random.standard_normal((B, H, S, D)) * G + A
    k = np.random.standard_normal((B, H, S, D)) * G - A
    v = np.random.standard_normal((B, H, S, D))
    q[..., 0] = Q0
    k[..., 0] = 0.5 * np.random.standard_normal((B, H, S)) + np.log2(t)
    return {"query": bf(q), "key": bf(k), "value": bf(v / t[:, None])}


def reference(query, key, value):
    d = key.shape[-1]
    score = f64(query) @ f64(key).transpose(0, 1, 3, 2) / np.sqrt(d)
    attn = restricted_softmax(score)
    return mxq(attn, 3, "e4m3") @ mxq(f64(value), 2, "e4m3")

@@ -1,0 +1,216 @@
+import math
+from contextlib import ExitStack
+
+import concourse.bass as bass
+import concourse.mybir as mybir
+import concourse.tile as tile
+from concourse.masks import make_identity
+
+FLOPS = 2 * 2 * 16 * 1024 * 1024 * 128
+
+F32 = mybir.dt.float32
+BF16 = mybir.dt.bfloat16
+U32 = mybir.dt.uint32
+U8 = mybir.dt.uint8
+FP8X4 = mybir.dt.float8_e4m3fn_x4
+ALU = mybir.AluOpType
+AF = mybir.ActivationFunctionType
+
+MANUAL = False
+H = 16
+S = 1024
+D = 128
+P = 128
+NT = S // P
+NX = 3
+DVE_EVAC = (7,)
+
+
+def tile_attention_kernel(tc, query, key, value, out):
+    nc = tc.nc
+    scale = 1.0 / math.sqrt(D)
+    total = H * NT
+    with ExitStack() as ctx:
+        const = ctx.enter_context(tc.tile_pool(name="const", bufs=1))
+        raw = ctx.enter_context(tc.tile_pool(name="raw", bufs=3))
+        head = ctx.enter_context(tc.tile_pool(name="head", bufs=2))
+        work = ctx.enter_context(tc.tile_pool(name="work", bufs=3))
+        small = ctx.enter_context(tc.tile_pool(name="small", bufs=6))
+        ps_s = ctx.enter_context(tc.psum_pool(name="ps_s", bufs=3))
+        ps_t = ctx.enter_context(tc.psum_pool(name="ps_t", bufs=3))
+        ps_o = ctx.enter_context(tc.psum_pool(name="ps_o", bufs=2))
+        if MANUAL:
+            ctx.enter_context(tc.manual_schedule())
+
+        ident = const.tile([P, P], BF16, name="ident")
+        make_identity(nc, ident[:])
+        xs = []
+        for j in range(NX):
+            xj = const.tile([P, S + 1], F32, name="x%d" % j)
+            nc.vector.memset(xj[:, S : S + 1], 0.0)
+            xs.append(xj)
+
+        st = {}
+
+        def load(h):
+            q_raw = raw.tile([P, NT, D], BF16, name="q_raw")
+            k_raw = raw.tile([P, NT, D], BF16, name="k_raw")
+            v_raw = raw.tile([P, NT, D], BF16, name="v_raw")
+            nc.sync.dma_start(out=q_raw[:], in_=query[0, h].rearrange("(p t) d -> p t d", t=NT))
+            nc.sync.dma_start(
+                out=k_raw[:].rearrange("p (g t) d -> p g t d", g=2),
+                in_=key[0, h].rearrange("(g p t) d -> p g t d", g=2, t=4),
+            )
+            nc.sync.dma_start(
+                out=v_raw[:].rearrange("p (g t) d -> p g t d", g=2),
+                in_=value[0, h].rearrange("(g p t) d -> p g t d", g=2, t=4),
+            )
+            st[("raw", h)] = (q_raw, k_raw, v_raw)
+
+        def prep(h):
+            q_raw, k_raw, v_raw = st[("raw", h)]
+            kt_ps = ps_t.tile([P, S], BF16, name="xt")
+            for b in range(NT):
+                nc.tensor.transpose(kt_ps[:, b * P : (b + 1) * P], k_raw[:, b, :], ident[:])
+            kT = head.tile([P, S], BF16, name="kT")
+            nc.vector.tensor_copy(out=kT[:], in_=kt_ps[:])
+            qt_ps = ps_t.tile([P, S], BF16, name="xt")
+            for b in range(NT):
+                nc.tensor.transpose(qt_ps[:, b * P : (b + 1) * P], q_raw[:, b, :], ident[:])
+            qT = head.tile([P, S], BF16, name="qT")
+            nc.vector.tensor_copy(out=qT[:], in_=qt_ps[:])
+            v_grp = head.tile([P, S], BF16, name="v_grp", align_bytes=64)
+            nc.gpsimd.tensor_scalar(
+                out=v_grp[:].rearrange("p (g d t) -> p g d t", g=2, t=4),
+                in0=v_raw[:].rearrange("p (g t) d -> p g d t", g=2),
+                scalar1=1.0,
+                scalar2=0.0,
+                op0=ALU.mult,
+                op1=ALU.add,
+            )
+            v_codes = head.tile([P, S // 4], U32, name="v_codes", align_bytes=64)
+            v_scl = head.tile([P, S // 4], U8, name="v_scl", align_bytes=64)
+            nc.vector.quantize_mx(out=v_codes[:].bitcast(FP8X4), scales=v_scl[:], in_=v_grp[:])
+            st[("head", h)] = (qT, kT, v_codes, v_scl)
+
+        def stage_s(n):
+            h, t = divmod(n, NT)
+            qT, kT = st[("head", h)][0:2]
+            banks = []
+            for half in range(2):
+                s_ps = ps_s.tile([P, 512], F32, name="s_ps")
+                nc.tensor.matmul(
+                    out=s_ps[:],
+                    lhsT=qT[:, t * P : (t + 1) * P],
+                    rhs=kT[:, half * 512 : (half + 1) * 512],
+                    start=True,
+                    stop=True,
+                )
+                banks.append(s_ps)
+            st[("s", n)] = banks
+
+        def stage_x(n):
+            s0, s1 = st[("s", n)]
+            x = xs[n % NX]
+            b0 = small.tile([P, 1], F32, name="b0")
+            bias = small.tile([P, 1], F32, name="bias")
+            nc.vector.tensor_scalar(
+                out=x[:, 0:512], in0=s0[:], scalar1=-scale, scalar2=0.0,
+                op0=ALU.mult, op1=ALU.min, accum_out=b0[:, 0:1],
+            )
+            nc.vector.tensor_scalar(
+                out=x[:, 512:1024], in0=s1[:], scalar1=-scale, scalar2=b0[:, 0:1],
+                op0=ALU.mult, op1=ALU.min, accum_out=bias[:, 0:1],
+            )
+            st[("x", n)] = (x, bias)
+
+        def stage_e(n):
+            x, bias = st[("x", n)]
+            e = work.tile([P, S + 1], F32, name="e")
+            den = small.tile([P, 1], F32, name="den")
+            nc.scalar.activation(
+                out=e[:], in_=x[:], func=AF.Exp, bias=bias[:, 0:1], scale=-1.0, accum_out=den[:, 0:1]
+            )
+            st[("e", n)] = (e, den)
+
+        def stage_r(n):
+            e, den = st[("e", n)]
+            r = small.tile([P, 1], F32, name="r")
+            nc.vector.reciprocal(out=r[:], in_=den[:])
+            st[("r", n)] = (e, r)
+
+        def stage_n(n):
+            e, r = st[("r", n)]
+            attn = work.tile([P, S], BF16, name="attn")
+            nc.gpsimd.tensor_scalar(
+                out=attn[:], in0=e[:, 0:S], scalar1=r[:, 0:1], scalar2=0.0, op0=ALU.mult, op1=ALU.add
+            )
+            st[("n", n)] = attn
+
+        def stage_t(n):
+            attn = st[("n", n)]
+            xt = ps_t.tile([P, S], BF16, name="xt")
+            for b in range(NT):
+                nc.tensor.transpose(xt[:, b * P : (b + 1) * P], attn[:, b * P : (b + 1) * P], ident[:])
+            st[("t", n)] = xt
+
+        def stage_g(n):
+            xt = st[("t", n)]
+            grp = work.tile([P, S], BF16, name="grp", align_bytes=64)
+            dst = grp[:].rearrange("p (g q t) -> p g q t", g=2, t=4)
+            src = xt[:].rearrange("p (g t q) -> p g q t", g=2, t=4)
+            if n % NT in DVE_EVAC:
+                nc.vector.tensor_copy(out=dst, in_=src)
+            else:
+                nc.scalar.copy(out=dst, in_=src)
+            st[("g", n)] = grp
+
+        def stage_q(n):
+            grp = st[("g", n)]
+            codes = work.tile([P, S // 4], U32, name="codes", align_bytes=64)
+            scl = work.tile([P, S // 4], U8, name="scl", align_bytes=64)
+            nc.vector.quantize_mx(out=codes[:].bitcast(FP8X4), scales=scl[:], in_=grp[:])
+            st[("q", n)] = (codes, scl)
+
+        def stage_m(n):
+            h, t = divmod(n, NT)
+            codes, scl = st[("q", n)]
+            v_codes, v_scl = st[("head", h)][2:4]
+            j = t % 4
+            if j == 0:
+                st["o"] = ps_o.tile([P, 512], F32, name="o_ps")
+            o_ps = st["o"]
+            for g in range(2):
+                cols = slice(g * P, (g + 1) * P)
+                nc.tensor.matmul_mx(
+                    out=o_ps[:, j * P : (j + 1) * P],
+                    lhsT=codes[:, cols].bitcast(FP8X4),
+                    lhsT_scale=scl[:, cols],
+                    rhs=v_codes[:, cols].bitcast(FP8X4),
+                    rhs_scale=v_scl[:, cols],
+                    start=(g == 0),
+                    stop=(g == 1),
+                )
+            if j == 3:
+                o_sb = work.tile([P, 512], F32, name="o_sb")
+                nc.vector.tensor_copy(out=o_sb[:], in_=o_ps[:])
+                nc.sync.dma_start(
+                    out=out[0, h].rearrange("(p t) d -> p t d", t=NT)[:, t - 3 : t + 1, :],
+                    in_=o_sb[:].rearrange("p (t d) -> p t d", t=4),
+                )
+
+        load(0)
+        load(1)
+        prep(0)
+        stages = ((stage_s, -1), (stage_x, 0), (stage_e, 1), (stage_r, 1), (stage_n, 1),
+                  (stage_t, 2), (stage_g, 2), (stage_q, 3), (stage_m, 3))
+        for k in range(-1, total + 4):
+            for fn, lag in stages:
+                n = k - lag
+                if 0 <= n < total:
+                    fn(n)
+            h, t = divmod(k, NT)
+            if 0 <= k < total and t == 1 and h + 2 < H:
+                load(h + 2)
+            if 0 <= k < total and t == 4 and h + 1 < H:
+                prep(h + 1)

@@ -16,7 +16,7 @@ FP8X4 = mybir.dt.float8_e4m3fn_x4
 ALU = mybir.AluOpType
 AF = mybir.ActivationFunctionType
 
-MANUAL = False
+MANUAL = True
 H = 16
 S = 1024
 D = 128
@@ -36,9 +36,9 @@ def tile_attention_kernel(tc, query, key, value, out):
         head = ctx.enter_context(tc.tile_pool(name="head", bufs=2))
         work = ctx.enter_context(tc.tile_pool(name="work", bufs=3))
         small = ctx.enter_context(tc.tile_pool(name="small", bufs=6))
-        ps_s = ctx.enter_context(tc.psum_pool(name="ps_s", bufs=3))
+        ps_s = ctx.enter_context(tc.psum_pool(name="ps_s", bufs=4))
         ps_t = ctx.enter_context(tc.psum_pool(name="ps_t", bufs=3))
-        ps_o = ctx.enter_context(tc.psum_pool(name="ps_o", bufs=2))
+        ps_o = ctx.enter_context(tc.psum_pool(name="ps_o", bufs=1))
         if MANUAL:
             ctx.enter_context(tc.manual_schedule())
 
@@ -67,18 +67,26 @@ def tile_attention_kernel(tc, query, key, value, out):
             )
             st[("raw", h)] = (q_raw, k_raw, v_raw)
 
-        def prep(h):
-            q_raw, k_raw, v_raw = st[("raw", h)]
+        def prep_k(h):
+            k_raw = st[("raw", h)][1]
             kt_ps = ps_t.tile([P, S], BF16, name="xt")
             for b in range(NT):
                 nc.tensor.transpose(kt_ps[:, b * P : (b + 1) * P], k_raw[:, b, :], ident[:])
             kT = head.tile([P, S], BF16, name="kT")
             nc.vector.tensor_copy(out=kT[:], in_=kt_ps[:])
+            st[("kT", h)] = kT
+
+        def prep_q(h):
+            q_raw = st[("raw", h)][0]
             qt_ps = ps_t.tile([P, S], BF16, name="xt")
             for b in range(NT):
                 nc.tensor.transpose(qt_ps[:, b * P : (b + 1) * P], q_raw[:, b, :], ident[:])
             qT = head.tile([P, S], BF16, name="qT")
             nc.vector.tensor_copy(out=qT[:], in_=qt_ps[:])
+            st[("qT", h)] = qT
+
+        def prep_v1(h):
+            v_raw = st[("raw", h)][2]
             v_grp = head.tile([P, S], BF16, name="v_grp", align_bytes=64)
             nc.gpsimd.tensor_scalar(
                 out=v_grp[:].rearrange("p (g d t) -> p g d t", g=2, t=4),
@@ -88,14 +96,19 @@ def tile_attention_kernel(tc, query, key, value, out):
                 op0=ALU.mult,
                 op1=ALU.add,
             )
+            st[("v_grp", h)] = v_grp
+
+        def prep_v2(h):
+            v_grp = st[("v_grp", h)]
             v_codes = head.tile([P, S // 4], U32, name="v_codes", align_bytes=64)
             v_scl = head.tile([P, S // 4], U8, name="v_scl", align_bytes=64)
             nc.vector.quantize_mx(out=v_codes[:].bitcast(FP8X4), scales=v_scl[:], in_=v_grp[:])
-            st[("head", h)] = (qT, kT, v_codes, v_scl)
+            st[("v", h)] = (v_codes, v_scl)
 
         def stage_s(n):
             h, t = divmod(n, NT)
-            qT, kT = st[("head", h)][0:2]
+            qT = st[("qT", h)]
+            kT = st[("kT", h)]
             banks = []
             for half in range(2):
                 s_ps = ps_s.tile([P, 512], F32, name="s_ps")
@@ -175,7 +188,7 @@ def tile_attention_kernel(tc, query, key, value, out):
         def stage_m(n):
             h, t = divmod(n, NT)
             codes, scl = st[("q", n)]
-            v_codes, v_scl = st[("head", h)][2:4]
+            v_codes, v_scl = st[("v", h)]
             j = t % 4
             if j == 0:
                 st["o"] = ps_o.tile([P, 512], F32, name="o_ps")
@@ -201,16 +214,27 @@ def tile_attention_kernel(tc, query, key, value, out):
 
         load(0)
         load(1)
-        prep(0)
-        stages = ((stage_s, -1), (stage_x, 0), (stage_e, 1), (stage_r, 1), (stage_n, 1),
-                  (stage_t, 2), (stage_g, 2), (stage_q, 3), (stage_m, 3))
-        for k in range(-1, total + 4):
+        prep_k(0)
+        prep_q(0)
+        prep_v1(0)
+        prep_v2(0)
+        stages = ((stage_s, -1), (stage_x, 0), (stage_e, 1), (stage_q, 4), (stage_r, 1), (stage_n, 1),
+                  (stage_t, 2), (stage_g, 3), (stage_m, 5))
+        for k in range(-1, total + 6):
             for fn, lag in stages:
                 n = k - lag
                 if 0 <= n < total:
                     fn(n)
             h, t = divmod(k, NT)
-            if 0 <= k < total and t == 1 and h + 2 < H:
-                load(h + 2)
-            if 0 <= k < total and t == 4 and h + 1 < H:
-                prep(h + 1)
+            if 0 <= k < total:
+                if t == 1 and h + 2 < H:
+                    load(h + 2)
+                if h + 1 < H:
+                    if t == 2:
+                        prep_k(h + 1)
+                    if t == 4:
+                        prep_q(h + 1)
+                    if t == 5:
+                        prep_v1(h + 1)
+                    if t == 6:
+                        prep_v2(h + 1)

@@ -22,7 +22,7 @@ S = 1024
 D = 128
 P = 128
 NT = S // P
-NX = 3
+NX = 4
 DVE_EVAC = (7,)
 
 
@@ -33,9 +33,10 @@ def tile_attention_kernel(tc, query, key, value, out):
     with ExitStack() as ctx:
         const = ctx.enter_context(tc.tile_pool(name="const", bufs=1))
         raw = ctx.enter_context(tc.tile_pool(name="raw", bufs=3))
-        head = ctx.enter_context(tc.tile_pool(name="head", bufs=2))
+        head = ctx.enter_context(tc.tile_pool(name="head", bufs=3))
         work = ctx.enter_context(tc.tile_pool(name="work", bufs=3))
-        small = ctx.enter_context(tc.tile_pool(name="small", bufs=6))
+        deep = ctx.enter_context(tc.tile_pool(name="deep", bufs=4))
+        small = ctx.enter_context(tc.tile_pool(name="small", bufs=10))
         ps_s = ctx.enter_context(tc.psum_pool(name="ps_s", bufs=4))
         ps_t = ctx.enter_context(tc.psum_pool(name="ps_t", bufs=3))
         ps_o = ctx.enter_context(tc.psum_pool(name="ps_o", bufs=1))
@@ -72,8 +73,11 @@ def tile_attention_kernel(tc, query, key, value, out):
             kt_ps = ps_t.tile([P, S], BF16, name="xt")
             for b in range(NT):
                 nc.tensor.transpose(kt_ps[:, b * P : (b + 1) * P], k_raw[:, b, :], ident[:])
+            st[("kt_ps", h)] = kt_ps
+
+        def prep_k2(h):
             kT = head.tile([P, S], BF16, name="kT")
-            nc.vector.tensor_copy(out=kT[:], in_=kt_ps[:])
+            nc.vector.tensor_copy(out=kT[:], in_=st[("kt_ps", h)][:])
             st[("kT", h)] = kT
 
         def prep_q(h):
@@ -81,8 +85,11 @@ def tile_attention_kernel(tc, query, key, value, out):
             qt_ps = ps_t.tile([P, S], BF16, name="xt")
             for b in range(NT):
                 nc.tensor.transpose(qt_ps[:, b * P : (b + 1) * P], q_raw[:, b, :], ident[:])
+            st[("qt_ps", h)] = qt_ps
+
+        def prep_q2(h):
             qT = head.tile([P, S], BF16, name="qT")
-            nc.vector.tensor_copy(out=qT[:], in_=qt_ps[:])
+            nc.vector.tensor_copy(out=qT[:], in_=st[("qt_ps", h)][:])
             st[("qT", h)] = qT
 
         def prep_v1(h):
@@ -125,21 +132,25 @@ def tile_attention_kernel(tc, query, key, value, out):
         def stage_x(n):
             s0, s1 = st[("s", n)]
             x = xs[n % NX]
-            b0 = small.tile([P, 1], F32, name="b0")
-            bias = small.tile([P, 1], F32, name="bias")
+            bb = small.tile([P, 2], F32, name="bb")
             nc.vector.tensor_scalar(
                 out=x[:, 0:512], in0=s0[:], scalar1=-scale, scalar2=0.0,
-                op0=ALU.mult, op1=ALU.min, accum_out=b0[:, 0:1],
+                op0=ALU.mult, op1=ALU.min, accum_out=bb[:, 0:1],
             )
             nc.vector.tensor_scalar(
-                out=x[:, 512:1024], in0=s1[:], scalar1=-scale, scalar2=b0[:, 0:1],
-                op0=ALU.mult, op1=ALU.min, accum_out=bias[:, 0:1],
+                out=x[:, 512:1024], in0=s1[:], scalar1=-scale, scalar2=0.0,
+                op0=ALU.mult, op1=ALU.min, accum_out=bb[:, 1:2],
             )
-            st[("x", n)] = (x, bias)
+            st[("bb", n)] = bb
+
+        def stage_b(n):
+            bias = small.tile([P, 1], F32, name="bias")
+            nc.vector.tensor_reduce(out=bias[:], in_=st[("bb", n)][:], axis=mybir.AxisListType.X, op=ALU.min)
+            st[("x", n)] = (xs[n % NX], bias)
 
         def stage_e(n):
             x, bias = st[("x", n)]
-            e = work.tile([P, S + 1], F32, name="e")
+            e = deep.tile([P, S + 1], F32, name="e")
             den = small.tile([P, 1], F32, name="den")
             nc.scalar.activation(
                 out=e[:], in_=x[:], func=AF.Exp, bias=bias[:, 0:1], scale=-1.0, accum_out=den[:, 0:1]
@@ -154,7 +165,7 @@ def tile_attention_kernel(tc, query, key, value, out):
 
         def stage_n(n):
             e, r = st[("r", n)]
-            attn = work.tile([P, S], BF16, name="attn")
+            attn = deep.tile([P, S], BF16, name="attn")
             nc.gpsimd.tensor_scalar(
                 out=attn[:], in0=e[:, 0:S], scalar1=r[:, 0:1], scalar2=0.0, op0=ALU.mult, op1=ALU.add
             )
@@ -215,26 +226,22 @@ def tile_attention_kernel(tc, query, key, value, out):
         load(0)
         load(1)
         prep_k(0)
+        prep_k2(0)
         prep_q(0)
+        prep_q2(0)
         prep_v1(0)
         prep_v2(0)
-        stages = ((stage_s, -1), (stage_x, 0), (stage_e, 1), (stage_q, 4), (stage_r, 1), (stage_n, 1),
-                  (stage_t, 2), (stage_g, 3), (stage_m, 5))
-        for k in range(-1, total + 6):
+        stages = ((stage_s, -1), (stage_x, 0), (stage_q, 7), (stage_b, 0), (stage_e, 2), (stage_r, 3),
+                  (stage_n, 3), (stage_t, 5), (stage_g, 6), (stage_m, 8))
+        preps = (None, prep_k, prep_k2, prep_q, prep_q2, prep_v1, prep_v2, None)
+        for k in range(-1, total + 9):
             for fn, lag in stages:
                 n = k - lag
                 if 0 <= n < total:
                     fn(n)
             h, t = divmod(k, NT)
             if 0 <= k < total:
-                if t == 1 and h + 2 < H:
+                if t == 0 and h + 2 < H:
                     load(h + 2)
-                if h + 1 < H:
-                    if t == 2:
-                        prep_k(h + 1)
-                    if t == 4:
-                        prep_q(h + 1)
-                    if t == 5:
-                        prep_v1(h + 1)
-                    if t == 6:
-                        prep_v2(h + 1)
+                if h + 1 < H and preps[t] is not None:
+                    preps[t](h + 1)

@@ -23,7 +23,7 @@ D = 128
 P = 128
 NT = S // P
 NX = 4
-DVE_EVAC = (7,)
+NB = 4
 
 
 def tile_attention_kernel(tc, query, key, value, out):
@@ -33,9 +33,10 @@ def tile_attention_kernel(tc, query, key, value, out):
     with ExitStack() as ctx:
         const = ctx.enter_context(tc.tile_pool(name="const", bufs=1))
         raw = ctx.enter_context(tc.tile_pool(name="raw", bufs=3))
-        head = ctx.enter_context(tc.tile_pool(name="head", bufs=3))
+        head = ctx.enter_context(tc.tile_pool(name="head", bufs=4))
         work = ctx.enter_context(tc.tile_pool(name="work", bufs=3))
         deep = ctx.enter_context(tc.tile_pool(name="deep", bufs=4))
+        batch = ctx.enter_context(tc.tile_pool(name="batch", bufs=3))
         small = ctx.enter_context(tc.tile_pool(name="small", bufs=10))
         ps_s = ctx.enter_context(tc.psum_pool(name="ps_s", bufs=4))
         ps_t = ctx.enter_context(tc.psum_pool(name="ps_t", bufs=3))
@@ -71,8 +72,10 @@ def tile_attention_kernel(tc, query, key, value, out):
         def prep_k(h):
             k_raw = st[("raw", h)][1]
             kt_ps = ps_t.tile([P, S], BF16, name="xt")
-            for b in range(NT):
-                nc.tensor.transpose(kt_ps[:, b * P : (b + 1) * P], k_raw[:, b, :], ident[:])
+            for g in range(2):
+                for t in range(4):
+                    col = (t * 2 + g) * P
+                    nc.tensor.transpose(kt_ps[:, col : col + P], k_raw[:, g * 4 + t, :], ident[:])
             st[("kt_ps", h)] = kt_ps
 
         def prep_k2(h):
@@ -165,28 +168,41 @@ def tile_attention_kernel(tc, query, key, value, out):
 
         def stage_n(n):
             e, r = st[("r", n)]
-            attn = deep.tile([P, S], BF16, name="attn")
+            b, i = divmod(n, NB)
+            if i == 0:
+                st[("attn", b)] = batch.tile([P, NB, S], BF16, name="attn")
             nc.gpsimd.tensor_scalar(
-                out=attn[:], in0=e[:, 0:S], scalar1=r[:, 0:1], scalar2=0.0, op0=ALU.mult, op1=ALU.add
+                out=st[("attn", b)][:, i, :], in0=e[:, 0:S], scalar1=r[:, 0:1], scalar2=0.0,
+                op0=ALU.mult, op1=ALU.add,
             )
-            st[("n", n)] = attn
+
+        def stage_d(n):
+            b, i = divmod(n, NB)
+            if i != NB - 1:
+                return
+            attn = st[("attn", b)]
+            z = batch.tile([P, NB, 4, 256], BF16, name="z")
+            for t in range(4):
+                for j in range(4):
+                    nc.sync.dma_start(
+                        out=z[t:P:4, :, j, :],
+                        in_=attn[32 * j : 32 * (j + 1), :, 256 * t : 256 * (t + 1)],
+                    )
+            st[("z", b)] = z
 
         def stage_t(n):
-            attn = st[("n", n)]
+            b, i = divmod(n, NB)
+            z = st[("z", b)]
             xt = ps_t.tile([P, S], BF16, name="xt")
-            for b in range(NT):
-                nc.tensor.transpose(xt[:, b * P : (b + 1) * P], attn[:, b * P : (b + 1) * P], ident[:])
+            for g in range(2):
+                for j in range(4):
+                    col = g * 512 + j * P
+                    nc.tensor.transpose(xt[:, col : col + P], z[:, i, j, g * P : (g + 1) * P], ident[:])
             st[("t", n)] = xt
 
         def stage_g(n):
-            xt = st[("t", n)]
             grp = work.tile([P, S], BF16, name="grp", align_bytes=64)
-            dst = grp[:].rearrange("p (g q t) -> p g q t", g=2, t=4)
-            src = xt[:].rearrange("p (g t q) -> p g q t", g=2, t=4)
-            if n % NT in DVE_EVAC:
-                nc.vector.tensor_copy(out=dst, in_=src)
-            else:
-                nc.scalar.copy(out=dst, in_=src)
+            nc.scalar.copy(out=grp[:], in_=st[("t", n)][:])
             st[("g", n)] = grp
 
         def stage_q(n):
@@ -217,7 +233,7 @@ def tile_attention_kernel(tc, query, key, value, out):
                 )
             if j == 3:
                 o_sb = work.tile([P, 512], F32, name="o_sb")
-                nc.vector.tensor_copy(out=o_sb[:], in_=o_ps[:])
+                nc.scalar.copy(out=o_sb[:], in_=o_ps[:])
                 nc.sync.dma_start(
                     out=out[0, h].rearrange("(p t) d -> p t d", t=NT)[:, t - 3 : t + 1, :],
                     in_=o_sb[:].rearrange("p (t d) -> p t d", t=4),
@@ -231,10 +247,10 @@ def tile_attention_kernel(tc, query, key, value, out):
         prep_q2(0)
         prep_v1(0)
         prep_v2(0)
-        stages = ((stage_s, -1), (stage_x, 0), (stage_q, 7), (stage_b, 0), (stage_e, 2), (stage_r, 3),
-                  (stage_n, 3), (stage_t, 5), (stage_g, 6), (stage_m, 8))
+        stages = ((stage_s, -1), (stage_x, 0), (stage_q, 15), (stage_b, 0), (stage_e, 2), (stage_r, 3),
+                  (stage_n, 3), (stage_d, 5), (stage_t, 13), (stage_g, 14), (stage_m, 16))
         preps = (None, prep_k, prep_k2, prep_q, prep_q2, prep_v1, prep_v2, None)
-        for k in range(-1, total + 9):
+        for k in range(-1, total + 17):
             for fn, lag in stages:
                 n = k - lag
                 if 0 <= n < total:

@@ -24,6 +24,7 @@ P = 128
 NT = S // P
 NX = 4
 NB = 4
+DVE_COPY = (1, 4, 7)
 
 
 def tile_attention_kernel(tc, query, key, value, out):
@@ -46,6 +47,10 @@ def tile_attention_kernel(tc, query, key, value, out):
 
         ident = const.tile([P, P], BF16, name="ident")
         make_identity(nc, ident[:])
+        perm = const.tile([P, P], BF16, name="perm")
+        nc.vector.tensor_copy(
+            out=perm[:].rearrange("p (a j) -> p a j", j=4), in_=ident[:].rearrange("p (j a) -> p a j", j=4)
+        )
         xs = []
         for j in range(NX):
             xj = const.tile([P, S + 1], F32, name="x%d" % j)
@@ -87,7 +92,7 @@ def tile_attention_kernel(tc, query, key, value, out):
             q_raw = st[("raw", h)][0]
             qt_ps = ps_t.tile([P, S], BF16, name="xt")
             for b in range(NT):
-                nc.tensor.transpose(qt_ps[:, b * P : (b + 1) * P], q_raw[:, b, :], ident[:])
+                nc.tensor.transpose(qt_ps[:, b * P : (b + 1) * P], q_raw[:, b, :], perm[:])
             st[("qt_ps", h)] = qt_ps
 
         def prep_q2(h):
@@ -170,9 +175,10 @@ def tile_attention_kernel(tc, query, key, value, out):
             e, r = st[("r", n)]
             b, i = divmod(n, NB)
             if i == 0:
-                st[("attn", b)] = batch.tile([P, NB, S], BF16, name="attn")
+                st[("attn", b)] = batch.tile([P, 4, NB, 256], BF16, name="attn")
             nc.gpsimd.tensor_scalar(
-                out=st[("attn", b)][:, i, :], in0=e[:, 0:S], scalar1=r[:, 0:1], scalar2=0.0,
+                out=st[("attn", b)][:, :, i, :], in0=e[:, 0:S].rearrange("p (t c) -> p t c", t=4),
+                scalar1=r[:, 0:1], scalar2=0.0,
                 op0=ALU.mult, op1=ALU.add,
             )
 
@@ -181,12 +187,12 @@ def tile_attention_kernel(tc, query, key, value, out):
             if i != NB - 1:
                 return
             attn = st[("attn", b)]
-            z = batch.tile([P, NB, 4, 256], BF16, name="z")
+            z = batch.tile([P, 4, NB, 256], BF16, name="z")
             for t in range(4):
                 for j in range(4):
                     nc.sync.dma_start(
-                        out=z[t:P:4, :, j, :],
-                        in_=attn[32 * j : 32 * (j + 1), :, 256 * t : 256 * (t + 1)],
+                        out=z[t:P:4, j, :, :],
+                        in_=attn[j:P:4, t, :, :],
                     )
             st[("z", b)] = z
 
@@ -197,12 +203,15 @@ def tile_attention_kernel(tc, query, key, value, out):
             for g in range(2):
                 for j in range(4):
                     col = g * 512 + j * P
-                    nc.tensor.transpose(xt[:, col : col + P], z[:, i, j, g * P : (g + 1) * P], ident[:])
+                    nc.tensor.transpose(xt[:, col : col + P], z[:, j, i, g * P : (g + 1) * P], ident[:])
             st[("t", n)] = xt
 
         def stage_g(n):
             grp = work.tile([P, S], BF16, name="grp", align_bytes=64)
-            nc.scalar.copy(out=grp[:], in_=st[("t", n)][:])
+            if n % NT in DVE_COPY:
+                nc.vector.tensor_copy(out=grp[:], in_=st[("t", n)][:])
+            else:
+                nc.scalar.copy(out=grp[:], in_=st[("t", n)][:])
             st[("g", n)] = grp
 
         def stage_q(n):

@@ -23,8 +23,8 @@ D = 128
 P = 128
 NT = S // P
 NX = 4
-NB = 4
-DVE_COPY = (1, 4, 7)
+NB = 8
+DVE_COPY = ()
 
 
 def tile_attention_kernel(tc, query, key, value, out):
@@ -34,7 +34,8 @@ def tile_attention_kernel(tc, query, key, value, out):
     with ExitStack() as ctx:
         const = ctx.enter_context(tc.tile_pool(name="const", bufs=1))
         raw = ctx.enter_context(tc.tile_pool(name="raw", bufs=3))
-        head = ctx.enter_context(tc.tile_pool(name="head", bufs=4))
+        head = ctx.enter_context(tc.tile_pool(name="head", bufs=3))
+        headv = ctx.enter_context(tc.tile_pool(name="headv", bufs=5))
         work = ctx.enter_context(tc.tile_pool(name="work", bufs=3))
         deep = ctx.enter_context(tc.tile_pool(name="deep", bufs=4))
         batch = ctx.enter_context(tc.tile_pool(name="batch", bufs=3))
@@ -102,7 +103,7 @@ def tile_attention_kernel(tc, query, key, value, out):
 
         def prep_v1(h):
             v_raw = st[("raw", h)][2]
-            v_grp = head.tile([P, S], BF16, name="v_grp", align_bytes=64)
+            v_grp = headv.tile([P, S], BF16, name="v_grp", align_bytes=64)
             nc.gpsimd.tensor_scalar(
                 out=v_grp[:].rearrange("p (g d t) -> p g d t", g=2, t=4),
                 in0=v_raw[:].rearrange("p (g t) d -> p g d t", g=2),
@@ -115,8 +116,8 @@ def tile_attention_kernel(tc, query, key, value, out):
 
         def prep_v2(h):
             v_grp = st[("v_grp", h)]
-            v_codes = head.tile([P, S // 4], U32, name="v_codes", align_bytes=64)
-            v_scl = head.tile([P, S // 4], U8, name="v_scl", align_bytes=64)
+            v_codes = headv.tile([P, S // 4], U32, name="v_codes", align_bytes=64)
+            v_scl = headv.tile([P, S // 4], U8, name="v_scl", align_bytes=64)
             nc.vector.quantize_mx(out=v_codes[:].bitcast(FP8X4), scales=v_scl[:], in_=v_grp[:])
             st[("v", h)] = (v_codes, v_scl)
 
@@ -256,10 +257,10 @@ def tile_attention_kernel(tc, query, key, value, out):
         prep_q2(0)
         prep_v1(0)
         prep_v2(0)
-        stages = ((stage_s, -1), (stage_x, 0), (stage_q, 15), (stage_b, 0), (stage_e, 2), (stage_r, 3),
-                  (stage_n, 3), (stage_d, 5), (stage_t, 13), (stage_g, 14), (stage_m, 16))
+        stages = ((stage_s, -1), (stage_x, 0), (stage_q, 23), (stage_b, 0), (stage_e, 2), (stage_r, 3),
+                  (stage_n, 3), (stage_d, 5), (stage_t, 21), (stage_g, 22), (stage_m, 24))
         preps = (None, prep_k, prep_k2, prep_q, prep_q2, prep_v1, prep_v2, None)
-        for k in range(-1, total + 17):
+        for k in range(-1, total + 25):
             for fn, lag in stages:
                 n = k - lag
                 if 0 <= n < total:

@@ -23,8 +23,7 @@ D = 128
 P = 128
 NT = S // P
 NX = 4
-NB = 8
-DVE_COPY = ()
+DVE_EVAC = (7,)
 
 
 def tile_attention_kernel(tc, query, key, value, out):
@@ -35,10 +34,8 @@ def tile_attention_kernel(tc, query, key, value, out):
         const = ctx.enter_context(tc.tile_pool(name="const", bufs=1))
         raw = ctx.enter_context(tc.tile_pool(name="raw", bufs=3))
         head = ctx.enter_context(tc.tile_pool(name="head", bufs=3))
-        headv = ctx.enter_context(tc.tile_pool(name="headv", bufs=5))
         work = ctx.enter_context(tc.tile_pool(name="work", bufs=3))
         deep = ctx.enter_context(tc.tile_pool(name="deep", bufs=4))
-        batch = ctx.enter_context(tc.tile_pool(name="batch", bufs=3))
         small = ctx.enter_context(tc.tile_pool(name="small", bufs=10))
         ps_s = ctx.enter_context(tc.psum_pool(name="ps_s", bufs=4))
         ps_t = ctx.enter_context(tc.psum_pool(name="ps_t", bufs=3))
@@ -48,10 +45,6 @@ def tile_attention_kernel(tc, query, key, value, out):
 
         ident = const.tile([P, P], BF16, name="ident")
         make_identity(nc, ident[:])
-        perm = const.tile([P, P], BF16, name="perm")
-        nc.vector.tensor_copy(
-            out=perm[:].rearrange("p (a j) -> p a j", j=4), in_=ident[:].rearrange("p (j a) -> p a j", j=4)
-        )
         xs = []
         for j in range(NX):
             xj = const.tile([P, S + 1], F32, name="x%d" % j)
@@ -78,10 +71,8 @@ def tile_attention_kernel(tc, query, key, value, out):
         def prep_k(h):
             k_raw = st[("raw", h)][1]
             kt_ps = ps_t.tile([P, S], BF16, name="xt")
-            for g in range(2):
-                for t in range(4):
-                    col = (t * 2 + g) * P
-                    nc.tensor.transpose(kt_ps[:, col : col + P], k_raw[:, g * 4 + t, :], ident[:])
+            for b in range(NT):
+                nc.tensor.transpose(kt_ps[:, b * P : (b + 1) * P], k_raw[:, b, :], ident[:])
             st[("kt_ps", h)] = kt_ps
 
         def prep_k2(h):
@@ -93,7 +84,7 @@ def tile_attention_kernel(tc, query, key, value, out):
             q_raw = st[("raw", h)][0]
             qt_ps = ps_t.tile([P, S], BF16, name="xt")
             for b in range(NT):
-                nc.tensor.transpose(qt_ps[:, b * P : (b + 1) * P], q_raw[:, b, :], perm[:])
+                nc.tensor.transpose(qt_ps[:, b * P : (b + 1) * P], q_raw[:, b, :], ident[:])
             st[("qt_ps", h)] = qt_ps
 
         def prep_q2(h):
@@ -103,7 +94,7 @@ def tile_attention_kernel(tc, query, key, value, out):
 
         def prep_v1(h):
             v_raw = st[("raw", h)][2]
-            v_grp = headv.tile([P, S], BF16, name="v_grp", align_bytes=64)
+            v_grp = head.tile([P, S], BF16, name="v_grp", align_bytes=64)
             nc.gpsimd.tensor_scalar(
                 out=v_grp[:].rearrange("p (g d t) -> p g d t", g=2, t=4),
                 in0=v_raw[:].rearrange("p (g t) d -> p g d t", g=2),
@@ -116,8 +107,8 @@ def tile_attention_kernel(tc, query, key, value, out):
 
         def prep_v2(h):
             v_grp = st[("v_grp", h)]
-            v_codes = headv.tile([P, S // 4], U32, name="v_codes", align_bytes=64)
-            v_scl = headv.tile([P, S // 4], U8, name="v_scl", align_bytes=64)
+            v_codes = head.tile([P, S // 4], U32, name="v_codes", align_bytes=64)
+            v_scl = head.tile([P, S // 4], U8, name="v_scl", align_bytes=64)
             nc.vector.quantize_mx(out=v_codes[:].bitcast(FP8X4), scales=v_scl[:], in_=v_grp[:])
             st[("v", h)] = (v_codes, v_scl)
 
@@ -174,45 +165,28 @@ def tile_attention_kernel(tc, query, key, value, out):
 
         def stage_n(n):
             e, r = st[("r", n)]
-            b, i = divmod(n, NB)
-            if i == 0:
-                st[("attn", b)] = batch.tile([P, 4, NB, 256], BF16, name="attn")
+            attn = deep.tile([P, S], BF16, name="attn")
             nc.gpsimd.tensor_scalar(
-                out=st[("attn", b)][:, :, i, :], in0=e[:, 0:S].rearrange("p (t c) -> p t c", t=4),
-                scalar1=r[:, 0:1], scalar2=0.0,
-                op0=ALU.mult, op1=ALU.add,
+                out=attn[:], in0=e[:, 0:S], scalar1=r[:, 0:1], scalar2=0.0, op0=ALU.mult, op1=ALU.add
             )
-
-        def stage_d(n):
-            b, i = divmod(n, NB)
-            if i != NB - 1:
-                return
-            attn = st[("attn", b)]
-            z = batch.tile([P, 4, NB, 256], BF16, name="z")
-            for t in range(4):
-                for j in range(4):
-                    nc.sync.dma_start(
-                        out=z[t:P:4, j, :, :],
-                        in_=attn[j:P:4, t, :, :],
-                    )
-            st[("z", b)] = z
+            st[("n", n)] = attn
 
         def stage_t(n):
-            b, i = divmod(n, NB)
-            z = st[("z", b)]
+            attn = st[("n", n)]
             xt = ps_t.tile([P, S], BF16, name="xt")
-            for g in range(2):
-                for j in range(4):
-                    col = g * 512 + j * P
-                    nc.tensor.transpose(xt[:, col : col + P], z[:, j, i, g * P : (g + 1) * P], ident[:])
+            for b in range(NT):
+                nc.tensor.transpose(xt[:, b * P : (b + 1) * P], attn[:, b * P : (b + 1) * P], ident[:])
             st[("t", n)] = xt
 
         def stage_g(n):
+            xt = st[("t", n)]
             grp = work.tile([P, S], BF16, name="grp", align_bytes=64)
-            if n % NT in DVE_COPY:
-                nc.vector.tensor_copy(out=grp[:], in_=st[("t", n)][:])
+            dst = grp[:].rearrange("p (g q t) -> p g q t", g=2, t=4)
+            src = xt[:].rearrange("p (g t q) -> p g q t", g=2, t=4)
+            if n % NT in DVE_EVAC:
+                nc.vector.tensor_copy(out=dst, in_=src)
             else:
-                nc.scalar.copy(out=grp[:], in_=st[("t", n)][:])
+                nc.scalar.copy(out=dst, in_=src)
             st[("g", n)] = grp
 
         def stage_q(n):
@@ -243,7 +217,7 @@ def tile_attention_kernel(tc, query, key, value, out):
                 )
             if j == 3:
                 o_sb = work.tile([P, 512], F32, name="o_sb")
-                nc.scalar.copy(out=o_sb[:], in_=o_ps[:])
+                nc.vector.tensor_copy(out=o_sb[:], in_=o_ps[:])
                 nc.sync.dma_start(
                     out=out[0, h].rearrange("(p t) d -> p t d", t=NT)[:, t - 3 : t + 1, :],
                     in_=o_sb[:].rearrange("p (t d) -> p t d", t=4),
@@ -257,10 +231,10 @@ def tile_attention_kernel(tc, query, key, value, out):
         prep_q2(0)
         prep_v1(0)
         prep_v2(0)
-        stages = ((stage_s, -1), (stage_x, 0), (stage_q, 23), (stage_b, 0), (stage_e, 2), (stage_r, 3),
-                  (stage_n, 3), (stage_d, 5), (stage_t, 21), (stage_g, 22), (stage_m, 24))
+        stages = ((stage_s, -1), (stage_x, 0), (stage_e, 2), (stage_r, 3), (stage_q, 7), (stage_n, 3),
+                  (stage_b, 0), (stage_t, 5), (stage_g, 6), (stage_m, 8))
         preps = (None, prep_k, prep_k2, prep_q, prep_q2, prep_v1, prep_v2, None)
-        for k in range(-1, total + 25):
+        for k in range(-1, total + 9):
             for fn, lag in stages:
                 n = k - lag
                 if 0 <= n < total:

@@ -23,7 +23,7 @@ D = 128
 P = 128
 NT = S // P
 NX = 4
-DVE_EVAC = (7,)
+DVE_EVAC = ()
 
 
 def tile_attention_kernel(tc, query, key, value, out):
@@ -45,6 +45,8 @@ def tile_attention_kernel(tc, query, key, value, out):
 
         ident = const.tile([P, P], BF16, name="ident")
         make_identity(nc, ident[:])
+        ident_w = const.tile([P, P], F32, name="ident_w")
+        make_identity(nc, ident_w[:])
         xs = []
         for j in range(NX):
             xj = const.tile([P, S + 1], F32, name="x%d" % j)
@@ -77,7 +79,10 @@ def tile_attention_kernel(tc, query, key, value, out):
 
         def prep_k2(h):
             kT = head.tile([P, S], BF16, name="kT")
-            nc.vector.tensor_copy(out=kT[:], in_=st[("kt_ps", h)][:])
+            nc.vector.tensor_copy(
+                out=kT[:].rearrange("d (a p e) -> d a p e", a=4, e=2),
+                in_=st[("kt_ps", h)][:].rearrange("d (a e p) -> d a p e", a=4, e=2),
+            )
             st[("kT", h)] = kT
 
         def prep_q(h):
@@ -173,16 +178,17 @@ def tile_attention_kernel(tc, query, key, value, out):
 
         def stage_t(n):
             attn = st[("n", n)]
-            xt = ps_t.tile([P, S], BF16, name="xt")
-            for b in range(NT):
-                nc.tensor.transpose(xt[:, b * P : (b + 1) * P], attn[:, b * P : (b + 1) * P], ident[:])
+            xt = ps_t.tile([P, S // 2], F32, name="xt")
+            words = attn[:].bitcast(F32)
+            for b in range(NT // 2):
+                nc.tensor.transpose(xt[:, b * P : (b + 1) * P], words[:, b * P : (b + 1) * P], ident_w[:])
             st[("t", n)] = xt
 
         def stage_g(n):
             xt = st[("t", n)]
             grp = work.tile([P, S], BF16, name="grp", align_bytes=64)
-            dst = grp[:].rearrange("p (g q t) -> p g q t", g=2, t=4)
-            src = xt[:].rearrange("p (g t q) -> p g q t", g=2, t=4)
+            dst = grp[:].bitcast(F32).rearrange("p (g q u) -> p g q u", g=2, u=2)
+            src = xt[:].rearrange("p (g u q) -> p g q u", g=2, u=2)
             if n % NT in DVE_EVAC:
                 nc.vector.tensor_copy(out=dst, in_=src)
             else:

@@ -79,7 +79,7 @@ def tile_attention_kernel(tc, query, key, value, out):
 
         def prep_k2(h):
             kT = head.tile([P, S], BF16, name="kT")
-            nc.vector.tensor_copy(
+            nc.scalar.copy(
                 out=kT[:].rearrange("d (a p e) -> d a p e", a=4, e=2),
                 in_=st[("kt_ps", h)][:].rearrange("d (a e p) -> d a p e", a=4, e=2),
             )
@@ -100,13 +100,9 @@ def tile_attention_kernel(tc, query, key, value, out):
         def prep_v1(h):
             v_raw = st[("raw", h)][2]
             v_grp = head.tile([P, S], BF16, name="v_grp", align_bytes=64)
-            nc.gpsimd.tensor_scalar(
+            nc.vector.tensor_copy(
                 out=v_grp[:].rearrange("p (g d t) -> p g d t", g=2, t=4),
-                in0=v_raw[:].rearrange("p (g t) d -> p g d t", g=2),
-                scalar1=1.0,
-                scalar2=0.0,
-                op0=ALU.mult,
-                op1=ALU.add,
+                in_=v_raw[:].rearrange("p (g t) d -> p g d t", g=2),
             )
             st[("v_grp", h)] = v_grp
 
@@ -221,13 +217,24 @@ def tile_attention_kernel(tc, query, key, value, out):
                     start=(g == 0),
                     stop=(g == 1),
                 )
-            if j == 3:
-                o_sb = work.tile([P, 512], F32, name="o_sb")
-                nc.vector.tensor_copy(out=o_sb[:], in_=o_ps[:])
-                nc.sync.dma_start(
-                    out=out[0, h].rearrange("(p t) d -> p t d", t=NT)[:, t - 3 : t + 1, :],
-                    in_=o_sb[:].rearrange("p (t d) -> p t d", t=4),
-                )
+
+        def stage_f(n):
+            h, t = divmod(n, NT)
+            if t % 4 != 3:
+                return
+            o_sb = work.tile([P, 512], F32, name="o_sb")
+            nc.scalar.copy(out=o_sb[:], in_=st["o"][:])
+            nc.sync.dma_start(
+                out=out[0, h].rearrange("(p t) d -> p t d", t=NT)[:, t - 3 : t + 1, :],
+                in_=o_sb[:].rearrange("p (t d) -> p t d", t=4),
+            )
+
+        def stage_v(n):
+            h, t = divmod(n, NT)
+            if h + 1 < H and t == 5:
+                prep_v1(h + 1)
+            if h + 1 < H and t == 6:
+                prep_v2(h + 1)
 
         load(0)
         load(1)
@@ -237,10 +244,10 @@ def tile_attention_kernel(tc, query, key, value, out):
         prep_q2(0)
         prep_v1(0)
         prep_v2(0)
-        stages = ((stage_s, -1), (stage_x, 0), (stage_e, 2), (stage_r, 3), (stage_q, 7), (stage_n, 3),
-                  (stage_b, 0), (stage_t, 5), (stage_g, 6), (stage_m, 8))
-        preps = (None, prep_k, prep_k2, prep_q, prep_q2, prep_v1, prep_v2, None)
-        for k in range(-1, total + 9):
+        stages = ((stage_f, 9), (stage_s, -1), (stage_x, 0), (stage_v, 0), (stage_e, 2), (stage_r, 3), (stage_q, 7),
+                  (stage_n, 3), (stage_b, 0), (stage_t, 5), (stage_g, 6), (stage_m, 8))
+        preps = (None, prep_k, prep_k2, prep_q, prep_q2, None, None, None)
+        for k in range(-1, total + 10):
             for fn, lag in stages:
                 n = k - lag
                 if 0 <= n < total:

@@ -131,23 +131,24 @@ def tile_attention_kernel(tc, query, key, value, out):
             st[("s", n)] = banks
 
         def stage_x(n):
-            s0, s1 = st[("s", n)]
+            s0 = st[("s", n)][0]
             x = xs[n % NX]
-            bb = small.tile([P, 2], F32, name="bb")
+            half = small.tile([P, 1], F32, name="half")
             nc.vector.tensor_scalar(
                 out=x[:, 0:512], in0=s0[:], scalar1=-scale, scalar2=0.0,
-                op0=ALU.mult, op1=ALU.min, accum_out=bb[:, 0:1],
+                op0=ALU.mult, op1=ALU.min, accum_out=half[:, 0:1],
             )
-            nc.vector.tensor_scalar(
-                out=x[:, 512:1024], in0=s1[:], scalar1=-scale, scalar2=0.0,
-                op0=ALU.mult, op1=ALU.min, accum_out=bb[:, 1:2],
-            )
-            st[("bb", n)] = bb
+            st[("half", n)] = half
 
         def stage_b(n):
+            s1 = st[("s", n)][1]
+            x = xs[n % NX]
             bias = small.tile([P, 1], F32, name="bias")
-            nc.vector.tensor_reduce(out=bias[:], in_=st[("bb", n)][:], axis=mybir.AxisListType.X, op=ALU.min)
-            st[("x", n)] = (xs[n % NX], bias)
+            nc.vector.tensor_scalar(
+                out=x[:, 512:1024], in0=s1[:], scalar1=-scale, scalar2=st[("half", n)][:, 0:1],
+                op0=ALU.mult, op1=ALU.min, accum_out=bias[:, 0:1],
+            )
+            st[("x", n)] = (x, bias)
 
         def stage_e(n):
             x, bias = st[("x", n)]
@@ -223,7 +224,7 @@ def tile_attention_kernel(tc, query, key, value, out):
             if t % 4 != 3:
                 return
             o_sb = work.tile([P, 512], F32, name="o_sb")
-            nc.scalar.copy(out=o_sb[:], in_=st["o"][:])
+            nc.vector.tensor_copy(out=o_sb[:], in_=st["o"][:])
             nc.sync.dma_start(
                 out=out[0, h].rearrange("(p t) d -> p t d", t=NT)[:, t - 3 : t + 1, :],
                 in_=o_sb[:].rearrange("p (t d) -> p t d", t=4),

@@ -45,6 +45,10 @@ def tile_attention_kernel(tc, query, key, value, out):
 
         ident = const.tile([P, P], BF16, name="ident")
         make_identity(nc, ident[:])
+        perm = const.tile([P, P], BF16, name="perm")
+        nc.vector.tensor_copy(
+            out=perm[:].rearrange("i (pl e) -> i pl e", e=2), in_=ident[:].rearrange("i (e pl) -> i pl e", e=2)
+        )
         ident_w = const.tile([P, P], F32, name="ident_w")
         make_identity(nc, ident_w[:])
         xs = []
@@ -60,10 +64,10 @@ def tile_attention_kernel(tc, query, key, value, out):
             k_raw = raw.tile([P, NT, D], BF16, name="k_raw")
             v_raw = raw.tile([P, NT, D], BF16, name="v_raw")
             nc.sync.dma_start(out=q_raw[:], in_=query[0, h].rearrange("(p t) d -> p t d", t=NT))
-            nc.sync.dma_start(
-                out=k_raw[:].rearrange("p (g t) d -> p g t d", g=2),
-                in_=key[0, h].rearrange("(g p t) d -> p g t d", g=2, t=4),
-            )
+            k_rows = key[0, h].rearrange("(a pl t) d -> t pl a d", a=4, t=4)
+            for u in range(2):
+                for e in range(2):
+                    nc.sync.dma_start(out=k_raw[64 * e : 64 * e + 64, u::2, :], in_=k_rows[2 * u + e])
             nc.sync.dma_start(
                 out=v_raw[:].rearrange("p (g t) d -> p g t d", g=2),
                 in_=value[0, h].rearrange("(g p t) d -> p g t d", g=2, t=4),
@@ -73,16 +77,16 @@ def tile_attention_kernel(tc, query, key, value, out):
         def prep_k(h):
             k_raw = st[("raw", h)][1]
             kt_ps = ps_t.tile([P, S], BF16, name="xt")
-            for b in range(NT):
-                nc.tensor.transpose(kt_ps[:, b * P : (b + 1) * P], k_raw[:, b, :], ident[:])
+            for g in range(2):
+                for u in range(2):
+                    for ph in range(2):
+                        c = 4 * g + 2 * u + ph
+                        nc.tensor.transpose(kt_ps[:, c * P : (c + 1) * P], k_raw[:, 4 * g + 2 * ph + u, :], perm[:])
             st[("kt_ps", h)] = kt_ps
 
         def prep_k2(h):
             kT = head.tile([P, S], BF16, name="kT")
-            nc.scalar.copy(
-                out=kT[:].rearrange("d (a p e) -> d a p e", a=4, e=2),
-                in_=st[("kt_ps", h)][:].rearrange("d (a e p) -> d a p e", a=4, e=2),
-            )
+            nc.scalar.copy(out=kT[:], in_=st[("kt_ps", h)][:])
             st[("kT", h)] = kT
 
         def prep_q(h):
@@ -94,7 +98,7 @@ def tile_attention_kernel(tc, query, key, value, out):
 
         def prep_q2(h):
             qT = head.tile([P, S], BF16, name="qT")
-            nc.vector.tensor_copy(out=qT[:], in_=st[("qt_ps", h)][:])
+            nc.scalar.copy(out=qT[:], in_=st[("qt_ps", h)][:])
             st[("qT", h)] = qT
 
         def prep_v1(h):

@@ -43,6 +43,9 @@ def tile_attention_kernel(tc, query, key, value, out):
         if MANUAL:
             ctx.enter_context(tc.manual_schedule())
 
+        warm = small.tile([P, 2], F32, name="warm")
+        nc.vector.memset(warm[:, 0:1], 0.0)
+        nc.scalar.activation(out=warm[:, 1:2], in_=warm[:, 0:1], func=AF.Exp)
         ident = const.tile([P, P], BF16, name="ident")
         make_identity(nc, ident[:])
         perm = const.tile([P, P], BF16, name="perm")
@@ -172,9 +175,12 @@ def tile_attention_kernel(tc, query, key, value, out):
         def stage_n(n):
             e, r = st[("r", n)]
             attn = deep.tile([P, S], BF16, name="attn")
-            nc.gpsimd.tensor_scalar(
-                out=attn[:], in0=e[:, 0:S], scalar1=r[:, 0:1], scalar2=0.0, op0=ALU.mult, op1=ALU.add
-            )
+            if n >= total - 3:
+                nc.vector.tensor_scalar(out=attn[:], in0=e[:, 0:S], scalar1=r[:, 0:1], scalar2=None, op0=ALU.mult)
+            else:
+                nc.gpsimd.tensor_scalar(
+                    out=attn[:], in0=e[:, 0:S], scalar1=r[:, 0:1], scalar2=0.0, op0=ALU.mult, op1=ALU.add
+                )
             st[("n", n)] = attn
 
         def stage_t(n):
@@ -190,7 +196,7 @@ def tile_attention_kernel(tc, query, key, value, out):
             grp = work.tile([P, S], BF16, name="grp", align_bytes=64)
             dst = grp[:].bitcast(F32).rearrange("p (g q u) -> p g q u", g=2, u=2)
             src = xt[:].rearrange("p (g u q) -> p g q u", g=2, u=2)
-            if n % NT in DVE_EVAC:
+            if n >= total - 6 and n % 2 == 0:
                 nc.vector.tensor_copy(out=dst, in_=src)
             else:
                 nc.scalar.copy(out=dst, in_=src)

@@ -108,8 +108,8 @@ def tile_attention_kernel(tc, query, key, value, out):
             v_raw = st[("raw", h)][2]
             v_grp = head.tile([P, S], BF16, name="v_grp", align_bytes=64)
             nc.vector.tensor_copy(
-                out=v_grp[:].rearrange("p (g d t) -> p g d t", g=2, t=4),
-                in_=v_raw[:].rearrange("p (g t) d -> p g d t", g=2),
+                out=v_grp[:].rearrange("p (g c i t) -> p g c t i", g=2, i=4, t=4),
+                in_=v_raw[:].rearrange("p (g t) (c i) -> p g c t i", g=2, i=4),
             )
             st[("v_grp", h)] = v_grp
 

@@ -66,15 +66,19 @@ def tile_attention_kernel(tc, query, key, value, out):
             q_raw = raw.tile([P, NT, D], BF16, name="q_raw")
             k_raw = raw.tile([P, NT, D], BF16, name="k_raw")
             v_raw = raw.tile([P, NT, D], BF16, name="v_raw")
-            nc.sync.dma_start(out=q_raw[:], in_=query[0, h].rearrange("(p t) d -> p t d", t=NT))
+            q_rows = query[0, h].rearrange("(p t) d -> p t d", t=NT)
             k_rows = key[0, h].rearrange("(a pl t) d -> t pl a d", a=4, t=4)
             for u in range(2):
                 for e in range(2):
                     nc.sync.dma_start(out=k_raw[64 * e : 64 * e + 64, u::2, :], in_=k_rows[2 * u + e])
+            q_cut = NT // 2 if h == 0 else NT
+            nc.sync.dma_start(out=q_raw[:, 0:q_cut, :], in_=q_rows[:, 0:q_cut, :])
             nc.sync.dma_start(
                 out=v_raw[:].rearrange("p (g t) d -> p g t d", g=2),
                 in_=value[0, h].rearrange("(g p t) d -> p g t d", g=2, t=4),
             )
+            if q_cut < NT:
+                nc.sync.dma_start(out=q_raw[:, q_cut:NT, :], in_=q_rows[:, q_cut:NT, :])
             st[("raw", h)] = (q_raw, k_raw, v_raw)
 
         def prep_k(h):
@@ -120,22 +124,51 @@ def tile_attention_kernel(tc, query, key, value, out):
             nc.vector.quantize_mx(out=v_codes[:].bitcast(FP8X4), scales=v_scl[:], in_=v_grp[:])
             st[("v", h)] = (v_codes, v_scl)
 
-        def stage_s(n):
+        def score_half(n, half):
             h, t = divmod(n, NT)
-            qT = st[("qT", h)]
-            kT = st[("kT", h)]
-            banks = []
-            for half in range(2):
-                s_ps = ps_s.tile([P, 512], F32, name="s_ps")
-                nc.tensor.matmul(
-                    out=s_ps[:],
-                    lhsT=qT[:, t * P : (t + 1) * P],
-                    rhs=kT[:, half * 512 : (half + 1) * 512],
-                    start=True,
-                    stop=True,
-                )
-                banks.append(s_ps)
-            st[("s", n)] = banks
+            s_ps = ps_s.tile([P, 512], F32, name="s_ps")
+            nc.tensor.matmul(
+                out=s_ps[:],
+                lhsT=st[("qT", h)][:, t * P : (t + 1) * P],
+                rhs=st[("kT", h)][:, half * 512 : (half + 1) * 512],
+                start=True,
+                stop=True,
+            )
+            return s_ps
+
+        def stage_s(n):
+            st[("s", n)] = [score_half(n, 0), score_half(n, 1)]
+
+        def first_head():
+            q_raw, k_raw = st[("raw", 0)][0:2]
+            kT = head.tile([P, S], BF16, name="kT")
+            qT = head.tile([P, S], BF16, name="qT")
+            st[("kT", 0)] = kT
+            st[("qT", 0)] = qT
+
+            def k_half(g):
+                kt_ps = ps_t.tile([P, 512], BF16, name="xt")
+                for u in range(2):
+                    for ph in range(2):
+                        c = 2 * u + ph
+                        nc.tensor.transpose(kt_ps[:, c * P : (c + 1) * P], k_raw[:, 4 * g + 2 * ph + u, :], perm[:])
+                return kt_ps
+
+            kt0 = k_half(0)
+            q01 = ps_s.tile([P, 2 * P], BF16, name="s_ps")
+            for b in range(2):
+                nc.tensor.transpose(q01[:, b * P : (b + 1) * P], q_raw[:, b, :], ident[:])
+            kt1 = k_half(1)
+            nc.scalar.copy(out=kT[:, 0:512], in_=kt0[:])
+            nc.scalar.copy(out=qT[:, 0 : 2 * P], in_=q01[:])
+            nc.scalar.copy(out=kT[:, 512:1024], in_=kt1[:])
+            s0 = score_half(0, 0)
+            q27 = ps_t.tile([P, 6 * P], BF16, name="xt")
+            for b in range(6):
+                nc.tensor.transpose(q27[:, b * P : (b + 1) * P], q_raw[:, b + 2, :], ident[:])
+            nc.scalar.copy(out=qT[:, 2 * P : S], in_=q27[:])
+            st[("s", 0)] = [s0, score_half(0, 1)]
+            prep_v1(0)
 
         def stage_x(n):
             s0 = st[("s", n)][0]
@@ -242,6 +275,8 @@ def tile_attention_kernel(tc, query, key, value, out):
 
         def stage_v(n):
             h, t = divmod(n, NT)
+            if n == 0:
+                prep_v2(0)
             if h + 1 < H and t == 5:
                 prep_v1(h + 1)
             if h + 1 < H and t == 6:
@@ -249,16 +284,11 @@ def tile_attention_kernel(tc, query, key, value, out):
 
         load(0)
         load(1)
-        prep_k(0)
-        prep_k2(0)
-        prep_q(0)
-        prep_q2(0)
-        prep_v1(0)
-        prep_v2(0)
+        first_head()
         stages = ((stage_f, 9), (stage_s, -1), (stage_x, 0), (stage_v, 0), (stage_e, 2), (stage_r, 3), (stage_q, 7),
                   (stage_n, 3), (stage_b, 0), (stage_t, 5), (stage_g, 6), (stage_m, 8))
         preps = (None, prep_k, prep_k2, prep_q, prep_q2, None, None, None)
-        for k in range(-1, total + 10):
+        for k in range(total + 10):
             for fn, lag in stages:
                 n = k - lag
                 if 0 <= n < total:

@@ -43,6 +43,12 @@ def tile_attention_kernel(tc, query, key, value, out):
         if MANUAL:
             ctx.enter_context(tc.manual_schedule())
 
+        if 5:
+            zero = const.tile([P, 512], BF16, name="zero")
+            nc.vector.memset(zero[:], 0.0)
+            w_ps = ps_s.tile([P, 512], F32, name="s_ps")
+            for i in range(5):
+                nc.tensor.matmul(out=w_ps[:], lhsT=zero[:, 0:P], rhs=zero[:], start=True, stop=True)
         warm = small.tile([P, 2], F32, name="warm")
         nc.vector.memset(warm[:, 0:1], 0.0)
         nc.scalar.activation(out=warm[:, 1:2], in_=warm[:, 0:1], func=AF.Exp)
@@ -70,7 +76,7 @@ def tile_attention_kernel(tc, query, key, value, out):
             k_rows = key[0, h].rearrange("(a pl t) d -> t pl a d", a=4, t=4)
             for u in range(2):
                 for e in range(2):
-                    nc.sync.dma_start(out=k_raw[64 * e : 64 * e + 64, u::2, :], in_=k_rows[2 * u + e])
+                    nc.sync.dma_start(out=k_raw[64 * e : 64 * e + 64, 4 * u : 4 * u + 4, :], in_=k_rows[2 * u + e])
             q_cut = NT // 2 if h == 0 else NT
             nc.sync.dma_start(out=q_raw[:, 0:q_cut, :], in_=q_rows[:, 0:q_cut, :])
             nc.sync.dma_start(
@@ -88,7 +94,7 @@ def tile_attention_kernel(tc, query, key, value, out):
                 for u in range(2):
                     for ph in range(2):
                         c = 4 * g + 2 * u + ph
-                        nc.tensor.transpose(kt_ps[:, c * P : (c + 1) * P], k_raw[:, 4 * g + 2 * ph + u, :], perm[:])
+                        nc.tensor.transpose(kt_ps[:, c * P : (c + 1) * P], k_raw[:, 4 * u + 2 * g + ph, :], perm[:])
             st[("kt_ps", h)] = kt_ps
 
         def prep_k2(h):
@@ -151,7 +157,7 @@ def tile_attention_kernel(tc, query, key, value, out):
                 for u in range(2):
                     for ph in range(2):
                         c = 2 * u + ph
-                        nc.tensor.transpose(kt_ps[:, c * P : (c + 1) * P], k_raw[:, 4 * g + 2 * ph + u, :], perm[:])
+                        nc.tensor.transpose(kt_ps[:, c * P : (c + 1) * P], k_raw[:, 4 * u + 2 * g + ph, :], perm[:])
                 return kt_ps
 
             kt0 = k_half(0)
@@ -229,7 +235,7 @@ def tile_attention_kernel(tc, query, key, value, out):
             grp = work.tile([P, S], BF16, name="grp", align_bytes=64)
             dst = grp[:].bitcast(F32).rearrange("p (g q u) -> p g q u", g=2, u=2)
             src = xt[:].rearrange("p (g u q) -> p g q u", g=2, u=2)
-            if n >= total - 6 and n % 2 == 0:
+            if n in ():
                 nc.vector.tensor_copy(out=dst, in_=src)
             else:
                 nc.scalar.copy(out=dst, in_=src)
@@ -248,8 +254,8 @@ def tile_attention_kernel(tc, query, key, value, out):
             v_codes, v_scl = st[("v", h)]
             j = t % 4
             if j == 0:
-                st["o"] = ps_o.tile([P, 512], F32, name="o_ps")
-            o_ps = st["o"]
+                st[("o", n // 4)] = ps_s.tile([P, 512], F32, name="s_ps") if n // 4 in () else ps_o.tile([P, 512], F32, name="o_ps")
+            o_ps = st[("o", n // 4)]
             for g in range(2):
                 cols = slice(g * P, (g + 1) * P)
                 nc.tensor.matmul_mx(
@@ -264,13 +270,23 @@ def tile_attention_kernel(tc, query, key, value, out):
 
         def stage_f(n):
             h, t = divmod(n, NT)
-            if t % 4 != 3:
+            if n == total - 1:
+                first = t
+            elif n == total - 2:
+                first = t - 2
+            elif t % 4 == 3:
+                first = t - 3
+            else:
                 return
+            cols = slice((first % 4) * D, (t % 4 + 1) * D)
             o_sb = work.tile([P, 512], F32, name="o_sb")
-            nc.vector.tensor_copy(out=o_sb[:], in_=st["o"][:])
+            if n in ():
+                nc.scalar.copy(out=o_sb[:, cols], in_=st[("o", n // 4)][:, cols])
+            else:
+                nc.vector.tensor_copy(out=o_sb[:, cols], in_=st[("o", n // 4)][:, cols])
             nc.sync.dma_start(
-                out=out[0, h].rearrange("(p t) d -> p t d", t=NT)[:, t - 3 : t + 1, :],
-                in_=o_sb[:].rearrange("p (t d) -> p t d", t=4),
+                out=out[0, h].rearrange("(p t) d -> p t d", t=NT)[:, first : t + 1, :],
+                in_=o_sb[:, cols].rearrange("p (t d) -> p t d", d=D),
             )
 
         def stage_v(n):
@@ -285,16 +301,19 @@ def tile_attention_kernel(tc, query, key, value, out):
         load(0)
         load(1)
         first_head()
-        stages = ((stage_f, 9), (stage_s, -1), (stage_x, 0), (stage_v, 0), (stage_e, 2), (stage_r, 3), (stage_q, 7),
-                  (stage_n, 3), (stage_b, 0), (stage_t, 5), (stage_g, 6), (stage_m, 8))
+        steady = (("f", 9), ("s", -1), ("x", 0), ("v", 0), ("e", 2), ("r", 3), ("q", 7), ("n", 3), ("b", 0), ("t", 5), ("g", 6), ("m", 8))
+        drain = (("f", 9), ("e", 2), ("r", 3), ("q", 7), ("n", 3), ("t", 5), ("g", 6), ("m", 8))
         preps = (None, prep_k, prep_k2, prep_q, prep_q2, None, None, None)
+        fns = dict(f=stage_f, s=stage_s, x=stage_x, v=stage_v, e=stage_e, r=stage_r, q=stage_q, n=stage_n, b=stage_b, t=stage_t,
+                   g=stage_g, m=stage_m)
+        todo = dict(f=0, s=1, x=0, v=0, e=0, r=0, q=0, n=0, b=0, t=0, g=0, m=0)
         for k in range(total + 10):
-            for fn, lag in stages:
-                n = k - lag
-                if 0 <= n < total:
-                    fn(n)
+            for name, lag in steady if k < total else drain:
+                for n in range(todo[name], min(k - lag + 1, total)):
+                    fns[name](n)
+                    todo[name] = n + 1
             h, t = divmod(k, NT)
-            if 0 <= k < total:
+            if k < total:
                 if t == 0 and h + 2 < H:
                     load(h + 2)
                 if h + 1 < H and preps[t] is not None:

@@ -293,7 +293,7 @@ def tile_attention_kernel(tc, query, key, value, out):
             h, t = divmod(n, NT)
             if n == 0:
                 prep_v2(0)
-            if h + 1 < H and t == 5:
+            if h + 1 < H and t == 2:
                 prep_v1(h + 1)
             if h + 1 < H and t == 6:
                 prep_v2(h + 1)

@@ -114,14 +114,30 @@ def tile_attention_kernel(tc, query, key, value, out):
             nc.scalar.copy(out=qT[:], in_=st[("qt_ps", h)][:])
             st[("qT", h)] = qT
 
-        def prep_v1(h):
+        def v_group(h):
+            if ("v_grp", h) not in st:
+                st[("v_grp", h)] = head.tile([P, S], BF16, name="v_grp", align_bytes=64)
+            return st[("v_grp", h)]
+
+        def prep_v1(h, passes):
             v_raw = st[("raw", h)][2]
-            v_grp = head.tile([P, S], BF16, name="v_grp", align_bytes=64)
+            v_grp = v_group(h)
+            cols = slice(512 * passes[0], 512 * (passes[-1] + 1))
+            rows = slice(4 * passes[0], 4 * (passes[-1] + 1))
             nc.vector.tensor_copy(
-                out=v_grp[:].rearrange("p (g c i t) -> p g c t i", g=2, i=4, t=4),
-                in_=v_raw[:].rearrange("p (g t) (c i) -> p g c t i", g=2, i=4),
+                out=v_grp[:, cols].rearrange("p (g c i t) -> p g c t i", g=len(passes), i=4, t=4),
+                in_=v_raw[:, rows, :].rearrange("p (g t) (c i) -> p g c t i", t=4, i=4),
             )
-            st[("v_grp", h)] = v_grp
+
+        def prep_vg(h, part):
+            v_raw = st[("raw", h)][2]
+            v_grp = v_group(h)
+            cols = slice(512 + 256 * part, 768 + 256 * part)
+            nc.gpsimd.tensor_scalar(
+                out=v_grp[:, cols].rearrange("p (c t) -> p c t", t=4),
+                in0=v_raw[:, 4:8, 64 * part : 64 * part + 64].rearrange("p t c -> p c t"),
+                scalar1=1.0, scalar2=0.0, op0=ALU.mult, op1=ALU.add,
+            )
 
         def prep_v2(h):
             v_grp = st[("v_grp", h)]
@@ -174,7 +190,7 @@ def tile_attention_kernel(tc, query, key, value, out):
                 nc.tensor.transpose(q27[:, b * P : (b + 1) * P], q_raw[:, b + 2, :], ident[:])
             nc.scalar.copy(out=qT[:, 2 * P : S], in_=q27[:])
             st[("s", 0)] = [s0, score_half(0, 1)]
-            prep_v1(0)
+            prep_v1(0, (0, 1))
 
         def stage_x(n):
             s0 = st[("s", n)][0]
@@ -293,20 +309,25 @@ def tile_attention_kernel(tc, query, key, value, out):
             h, t = divmod(n, NT)
             if n == 0:
                 prep_v2(0)
+            if h > 0 and t == 2:
+                prep_v2(h)
             if h + 1 < H and t == 2:
-                prep_v1(h + 1)
-            if h + 1 < H and t == 6:
-                prep_v2(h + 1)
+                prep_v1(h + 1, (0,))
+
+        def stage_h(n):
+            h, t = divmod(n, NT)
+            if h + 1 < H and t % 4 == 3:
+                prep_vg(h + 1, t // 4)
 
         load(0)
         load(1)
         first_head()
-        steady = (("f", 9), ("s", -1), ("x", 0), ("v", 0), ("e", 2), ("r", 3), ("q", 7), ("n", 3), ("b", 0), ("t", 5), ("g", 6), ("m", 8))
+        steady = (("f", 9), ("s", -1), ("x", 0), ("v", 0), ("e", 2), ("r", 3), ("q", 7), ("n", 3), ("h", 0), ("b", 0), ("t", 5), ("g", 6), ("m", 8))
         drain = (("f", 9), ("e", 2), ("r", 3), ("q", 7), ("n", 3), ("t", 5), ("g", 6), ("m", 8))
         preps = (None, prep_k, prep_k2, prep_q, prep_q2, None, None, None)
         fns = dict(f=stage_f, s=stage_s, x=stage_x, v=stage_v, e=stage_e, r=stage_r, q=stage_q, n=stage_n, b=stage_b, t=stage_t,
-                   g=stage_g, m=stage_m)
-        todo = dict(f=0, s=1, x=0, v=0, e=0, r=0, q=0, n=0, b=0, t=0, g=0, m=0)
+                   g=stage_g, m=stage_m, h=stage_h)
+        todo = dict(f=0, s=1, x=0, v=0, e=0, r=0, q=0, n=0, b=0, t=0, g=0, m=0, h=0)
         for k in range(total + 10):
             for name, lag in steady if k < total else drain:
                 for n in range(todo[name], min(k - lag + 1, total)):

@@ -43,7 +43,7 @@ def tile_attention_kernel(tc, query, key, value, out):
         if MANUAL:
             ctx.enter_context(tc.manual_schedule())
 
-        if 5:
+        if True:
             zero = const.tile([P, 512], BF16, name="zero")
             nc.vector.memset(zero[:], 0.0)
             w_ps = ps_s.tile([P, 512], F32, name="s_ps")
@@ -119,23 +119,16 @@ def tile_attention_kernel(tc, query, key, value, out):
                 st[("v_grp", h)] = head.tile([P, S], BF16, name="v_grp", align_bytes=64)
             return st[("v_grp", h)]
 
-        def prep_v1(h, passes):
-            v_raw = st[("raw", h)][2]
-            v_grp = v_group(h)
-            cols = slice(512 * passes[0], 512 * (passes[-1] + 1))
-            rows = slice(4 * passes[0], 4 * (passes[-1] + 1))
+        def prep_v1(h):
             nc.vector.tensor_copy(
-                out=v_grp[:, cols].rearrange("p (g c i t) -> p g c t i", g=len(passes), i=4, t=4),
-                in_=v_raw[:, rows, :].rearrange("p (g t) (c i) -> p g c t i", t=4, i=4),
+                out=v_group(h)[:, 0:512].rearrange("p (c i t) -> p c t i", i=4, t=4),
+                in_=st[("raw", h)][2][:, 0:4, :].rearrange("p t (c i) -> p c t i", i=4),
             )
 
-        def prep_vg(h, part):
-            v_raw = st[("raw", h)][2]
-            v_grp = v_group(h)
-            cols = slice(512 + 256 * part, 768 + 256 * part)
+        def prep_vg(h, g, lo, hi):
             nc.gpsimd.tensor_scalar(
-                out=v_grp[:, cols].rearrange("p (c t) -> p c t", t=4),
-                in0=v_raw[:, 4:8, 64 * part : 64 * part + 64].rearrange("p t c -> p c t"),
+                out=v_group(h)[:, 512 * g + 4 * lo : 512 * g + 4 * hi].rearrange("p (c t) -> p c t", t=4),
+                in0=st[("raw", h)][2][:, 4 * g : 4 * g + 4, lo:hi].rearrange("p t c -> p c t"),
                 scalar1=1.0, scalar2=0.0, op0=ALU.mult, op1=ALU.add,
             )
 
@@ -182,15 +175,17 @@ def tile_attention_kernel(tc, query, key, value, out):
                 nc.tensor.transpose(q01[:, b * P : (b + 1) * P], q_raw[:, b, :], ident[:])
             kt1 = k_half(1)
             nc.scalar.copy(out=kT[:, 0:512], in_=kt0[:])
-            nc.scalar.copy(out=qT[:, 0 : 2 * P], in_=q01[:])
+            nc.vector.tensor_copy(out=qT[:, 0 : 2 * P], in_=q01[:])
             nc.scalar.copy(out=kT[:, 512:1024], in_=kt1[:])
-            s0 = score_half(0, 0)
+            stage_s(0)
+            for g in range(2):
+                prep_vg(0, g, 0, D)
+
+        def first_head_rest():
             q27 = ps_t.tile([P, 6 * P], BF16, name="xt")
             for b in range(6):
-                nc.tensor.transpose(q27[:, b * P : (b + 1) * P], q_raw[:, b + 2, :], ident[:])
-            nc.scalar.copy(out=qT[:, 2 * P : S], in_=q27[:])
-            st[("s", 0)] = [s0, score_half(0, 1)]
-            prep_v1(0, (0, 1))
+                nc.tensor.transpose(q27[:, b * P : (b + 1) * P], st[("raw", 0)][0][:, b + 2, :], ident[:])
+            nc.scalar.copy(out=st[("qT", 0)][:, 2 * P : S], in_=q27[:])
 
         def stage_x(n):
             s0 = st[("s", n)][0]
@@ -251,10 +246,7 @@ def tile_attention_kernel(tc, query, key, value, out):
             grp = work.tile([P, S], BF16, name="grp", align_bytes=64)
             dst = grp[:].bitcast(F32).rearrange("p (g q u) -> p g q u", g=2, u=2)
             src = xt[:].rearrange("p (g u q) -> p g q u", g=2, u=2)
-            if n in ():
-                nc.vector.tensor_copy(out=dst, in_=src)
-            else:
-                nc.scalar.copy(out=dst, in_=src)
+            nc.scalar.copy(out=dst, in_=src)
             st[("g", n)] = grp
 
         def stage_q(n):
@@ -269,9 +261,13 @@ def tile_attention_kernel(tc, query, key, value, out):
             codes, scl = st[("q", n)]
             v_codes, v_scl = st[("v", h)]
             j = t % 4
-            if j == 0:
-                st[("o", n // 4)] = ps_s.tile([P, 512], F32, name="s_ps") if n // 4 in () else ps_o.tile([P, 512], F32, name="o_ps")
-            o_ps = st[("o", n // 4)]
+            if n == total - 1:
+                o_ps = ps_s.tile([P, 512], F32, name="s_ps")
+            elif j == 0:
+                o_ps = ps_o.tile([P, 512], F32, name="o_ps")
+            else:
+                o_ps = st[("o", n - 1)]
+            st[("o", n)] = o_ps
             for g in range(2):
                 cols = slice(g * P, (g + 1) * P)
                 nc.tensor.matmul_mx(
@@ -296,10 +292,7 @@ def tile_attention_kernel(tc, query, key, value, out):
                 return
             cols = slice((first % 4) * D, (t % 4 + 1) * D)
             o_sb = work.tile([P, 512], F32, name="o_sb")
-            if n in ():
-                nc.scalar.copy(out=o_sb[:, cols], in_=st[("o", n // 4)][:, cols])
-            else:
-                nc.vector.tensor_copy(out=o_sb[:, cols], in_=st[("o", n // 4)][:, cols])
+            nc.vector.tensor_copy(out=o_sb[:, cols], in_=st[("o", n)][:, cols])
             nc.sync.dma_start(
                 out=out[0, h].rearrange("(p t) d -> p t d", t=NT)[:, first : t + 1, :],
                 in_=o_sb[:, cols].rearrange("p (t d) -> p t d", d=D),
@@ -307,17 +300,15 @@ def tile_attention_kernel(tc, query, key, value, out):
 
         def stage_v(n):
             h, t = divmod(n, NT)
-            if n == 0:
-                prep_v2(0)
-            if h > 0 and t == 2:
+            if t == 1:
                 prep_v2(h)
             if h + 1 < H and t == 2:
-                prep_v1(h + 1, (0,))
+                prep_v1(h + 1)
 
         def stage_h(n):
             h, t = divmod(n, NT)
             if h + 1 < H and t % 4 == 3:
-                prep_vg(h + 1, t // 4)
+                prep_vg(h + 1, 1, 64 * (t // 4), 64 * (t // 4) + 64)
 
         load(0)
         load(1)
@@ -334,6 +325,8 @@ def tile_attention_kernel(tc, query, key, value, out):
                     fns[name](n)
                     todo[name] = n + 1
             h, t = divmod(k, NT)
+            if k == 0:
+                first_head_rest()
             if k < total:
                 if t == 0 and h + 2 < H:
                     load(h + 2)

@@ -313,7 +313,7 @@ def tile_attention_kernel(tc, query, key, value, out):
         load(0)
         load(1)
         first_head()
-        steady = (("f", 9), ("s", -1), ("x", 0), ("v", 0), ("e", 2), ("r", 3), ("q", 7), ("n", 3), ("h", 0), ("b", 0), ("t", 5), ("g", 6), ("m", 8))
+        steady = (("f", 9), ("t", 5), ("s", -1), ("x", 0), ("v", 0), ("e", 2), ("r", 3), ("q", 7), ("n", 3), ("h", 0), ("b", 0), ("g", 6), ("m", 8))
         drain = (("f", 9), ("e", 2), ("r", 3), ("q", 7), ("n", 3), ("t", 5), ("g", 6), ("m", 8))
         preps = (None, prep_k, prep_k2, prep_q, prep_q2, None, None, None)
         fns = dict(f=stage_f, s=stage_s, x=stage_x, v=stage_v, e=stage_e, r=stage_r, q=stage_q, n=stage_n, b=stage_b, t=stage_t,

@@ -302,7 +302,7 @@ def tile_attention_kernel(tc, query, key, value, out):
             h, t = divmod(n, NT)
             if t == 1:
                 prep_v2(h)
-            if h + 1 < H and t == 2:
+            if h + 1 < H and t == 1:
                 prep_v1(h + 1)
 
         def stage_h(n):

import math
from contextlib import ExitStack

import concourse.bass as bass
import concourse.mybir as mybir
import concourse.tile as tile
from concourse.masks import make_identity

FLOPS = 2 * 2 * 16 * 1024 * 1024 * 128

F32 = mybir.dt.float32
BF16 = mybir.dt.bfloat16
U32 = mybir.dt.uint32
U8 = mybir.dt.uint8
FP8X4 = mybir.dt.float8_e4m3fn_x4
ALU = mybir.AluOpType
AF = mybir.ActivationFunctionType

MANUAL = True
H = 16
S = 1024
D = 128
P = 128
NT = S // P
NX = 4
DVE_EVAC = ()


def tile_attention_kernel(tc, query, key, value, out):
    nc = tc.nc
    scale = 1.0 / math.sqrt(D)
    total = H * NT
    with ExitStack() as ctx:
        const = ctx.enter_context(tc.tile_pool(name="const", bufs=1))
        raw = ctx.enter_context(tc.tile_pool(name="raw", bufs=3))
        head = ctx.enter_context(tc.tile_pool(name="head", bufs=3))
        work = ctx.enter_context(tc.tile_pool(name="work", bufs=3))
        deep = ctx.enter_context(tc.tile_pool(name="deep", bufs=4))
        small = ctx.enter_context(tc.tile_pool(name="small", bufs=10))
        ps_s = ctx.enter_context(tc.psum_pool(name="ps_s", bufs=4))
        ps_t = ctx.enter_context(tc.psum_pool(name="ps_t", bufs=3))
        ps_o = ctx.enter_context(tc.psum_pool(name="ps_o", bufs=1))
        if MANUAL:
            ctx.enter_context(tc.manual_schedule())

        if True:
            zero = const.tile([P, 512], BF16, name="zero")
            nc.vector.memset(zero[:], 0.0)
            w_ps = ps_s.tile([P, 512], F32, name="s_ps")
            for i in range(5):
                nc.tensor.matmul(out=w_ps[:], lhsT=zero[:, 0:P], rhs=zero[:], start=True, stop=True)
        warm = small.tile([P, 2], F32, name="warm")
        nc.vector.memset(warm[:, 0:1], 0.0)
        nc.scalar.activation(out=warm[:, 1:2], in_=warm[:, 0:1], func=AF.Exp)
        ident = const.tile([P, P], BF16, name="ident")
        make_identity(nc, ident[:])
        perm = const.tile([P, P], BF16, name="perm")
        nc.vector.tensor_copy(
            out=perm[:].rearrange("i (pl e) -> i pl e", e=2), in_=ident[:].rearrange("i (e pl) -> i pl e", e=2)
        )
        ident_w = const.tile([P, P], F32, name="ident_w")
        make_identity(nc, ident_w[:])
        xs = []
        for j in range(NX):
            xj = const.tile([P, S + 1], F32, name="x%d" % j)
            nc.vector.memset(xj[:, S : S + 1], 0.0)
            xs.append(xj)

        st = {}

        def load(h):
            q_raw = raw.tile([P, NT, D], BF16, name="q_raw")
            k_raw = raw.tile([P, NT, D], BF16, name="k_raw")
            v_raw = raw.tile([P, NT, D], BF16, name="v_raw")
            q_rows = query[0, h].rearrange("(p t) d -> p t d", t=NT)
            k_rows = key[0, h].rearrange("(a pl t) d -> t pl a d", a=4, t=4)
            for u in range(2):
                for e in range(2):
                    nc.sync.dma_start(out=k_raw[64 * e : 64 * e + 64, 4 * u : 4 * u + 4, :], in_=k_rows[2 * u + e])
            q_cut = NT // 2 if h == 0 else NT
            nc.sync.dma_start(out=q_raw[:, 0:q_cut, :], in_=q_rows[:, 0:q_cut, :])
            nc.sync.dma_start(
                out=v_raw[:].rearrange("p (g t) d -> p g t d", g=2),
                in_=value[0, h].rearrange("(g p t) d -> p g t d", g=2, t=4),
            )
            if q_cut < NT:
                nc.sync.dma_start(out=q_raw[:, q_cut:NT, :], in_=q_rows[:, q_cut:NT, :])
            st[("raw", h)] = (q_raw, k_raw, v_raw)

        def prep_k(h):
            k_raw = st[("raw", h)][1]
            kt_ps = ps_t.tile([P, S], BF16, name="xt")
            for g in range(2):
                for u in range(2):
                    for ph in range(2):
                        c = 4 * g + 2 * u + ph
                        nc.tensor.transpose(kt_ps[:, c * P : (c + 1) * P], k_raw[:, 4 * u + 2 * g + ph, :], perm[:])
            st[("kt_ps", h)] = kt_ps

        def prep_k2(h):
            kT = head.tile([P, S], BF16, name="kT")
            nc.scalar.copy(out=kT[:], in_=st[("kt_ps", h)][:])
            st[("kT", h)] = kT

        def prep_q(h):
            q_raw = st[("raw", h)][0]
            qt_ps = ps_t.tile([P, S], BF16, name="xt")
            for b in range(NT):
                nc.tensor.transpose(qt_ps[:, b * P : (b + 1) * P], q_raw[:, b, :], ident[:])
            st[("qt_ps", h)] = qt_ps

        def prep_q2(h):
            qT = head.tile([P, S], BF16, name="qT")
            nc.scalar.copy(out=qT[:], in_=st[("qt_ps", h)][:])
            st[("qT", h)] = qT

        def v_group(h):
            if ("v_grp", h) not in st:
                st[("v_grp", h)] = head.tile([P, S], BF16, name="v_grp", align_bytes=64)
            return st[("v_grp", h)]

        def prep_v1(h):
            nc.vector.tensor_copy(
                out=v_group(h)[:, 0:512].rearrange("p (c i t) -> p c t i", i=4, t=4),
                in_=st[("raw", h)][2][:, 0:4, :].rearrange("p t (c i) -> p c t i", i=4),
            )

        def prep_vg(h, g, lo, hi):
            nc.gpsimd.tensor_scalar(
                out=v_group(h)[:, 512 * g + 4 * lo : 512 * g + 4 * hi].rearrange("p (c t) -> p c t", t=4),
                in0=st[("raw", h)][2][:, 4 * g : 4 * g + 4, lo:hi].rearrange("p t c -> p c t"),
                scalar1=1.0, scalar2=0.0, op0=ALU.mult, op1=ALU.add,
            )

        def prep_v2(h):
            v_grp = st[("v_grp", h)]
            v_codes = head.tile([P, S // 4], U32, name="v_codes", align_bytes=64)
            v_scl = head.tile([P, S // 4], U8, name="v_scl", align_bytes=64)
            nc.vector.quantize_mx(out=v_codes[:].bitcast(FP8X4), scales=v_scl[:], in_=v_grp[:])
            st[("v", h)] = (v_codes, v_scl)

        def score_half(n, half):
            h, t = divmod(n, NT)
            s_ps = ps_s.tile([P, 512], F32, name="s_ps")
            nc.tensor.matmul(
                out=s_ps[:],
                lhsT=st[("qT", h)][:, t * P : (t + 1) * P],
                rhs=st[("kT", h)][:, half * 512 : (half + 1) * 512],
                start=True,
                stop=True,
            )
            return s_ps

        def stage_s(n):
            st[("s", n)] = [score_half(n, 0), score_half(n, 1)]

        def first_head():
            q_raw, k_raw = st[("raw", 0)][0:2]
            kT = head.tile([P, S], BF16, name="kT")
            qT = head.tile([P, S], BF16, name="qT")
            st[("kT", 0)] = kT
            st[("qT", 0)] = qT

            def k_half(g):
                kt_ps = ps_t.tile([P, 512], BF16, name="xt")
                for u in range(2):
                    for ph in range(2):
                        c = 2 * u + ph
                        nc.tensor.transpose(kt_ps[:, c * P : (c + 1) * P], k_raw[:, 4 * u + 2 * g + ph, :], perm[:])
                return kt_ps

            kt0 = k_half(0)
            q01 = ps_s.tile([P, 2 * P], BF16, name="s_ps")
            for b in range(2):
                nc.tensor.transpose(q01[:, b * P : (b + 1) * P], q_raw[:, b, :], ident[:])
            kt1 = k_half(1)
            nc.scalar.copy(out=kT[:, 0:512], in_=kt0[:])
            nc.vector.tensor_copy(out=qT[:, 0 : 2 * P], in_=q01[:])
            nc.scalar.copy(out=kT[:, 512:1024], in_=kt1[:])
            stage_s(0)
            for g in range(2):
                prep_vg(0, g, 0, D)

        def first_head_rest():
            q27 = ps_t.tile([P, 6 * P], BF16, name="xt")
            for b in range(6):
                nc.tensor.transpose(q27[:, b * P : (b + 1) * P], st[("raw", 0)][0][:, b + 2, :], ident[:])
            nc.scalar.copy(out=st[("qT", 0)][:, 2 * P : S], in_=q27[:])

        def stage_x(n):
            s0 = st[("s", n)][0]
            x = xs[n % NX]
            half = small.tile([P, 1], F32, name="half")
            nc.vector.tensor_scalar(
                out=x[:, 0:512], in0=s0[:], scalar1=-scale, scalar2=0.0,
                op0=ALU.mult, op1=ALU.min, accum_out=half[:, 0:1],
            )
            st[("half", n)] = half

        def stage_b(n):
            s1 = st[("s", n)][1]
            x = xs[n % NX]
            bias = small.tile([P, 1], F32, name="bias")
            nc.vector.tensor_scalar(
                out=x[:, 512:1024], in0=s1[:], scalar1=-scale, scalar2=st[("half", n)][:, 0:1],
                op0=ALU.mult, op1=ALU.min, accum_out=bias[:, 0:1],
            )
            st[("x", n)] = (x, bias)

        def stage_e(n):
            x, bias = st[("x", n)]
            e = deep.tile([P, S + 1], F32, name="e")
            den = small.tile([P, 1], F32, name="den")
            nc.scalar.activation(
                out=e[:], in_=x[:], func=AF.Exp, bias=bias[:, 0:1], scale=-1.0, accum_out=den[:, 0:1]
            )
            st[("e", n)] = (e, den)

        def stage_r(n):
            e, den = st[("e", n)]
            r = small.tile([P, 1], F32, name="r")
            nc.vector.reciprocal(out=r[:], in_=den[:])
            st[("r", n)] = (e, r)

        def stage_n(n):
            e, r = st[("r", n)]
            attn = deep.tile([P, S], BF16, name="attn")
            if n >= total - 3:
                nc.vector.tensor_scalar(out=attn[:], in0=e[:, 0:S], scalar1=r[:, 0:1], scalar2=None, op0=ALU.mult)
            else:
                nc.gpsimd.tensor_scalar(
                    out=attn[:], in0=e[:, 0:S], scalar1=r[:, 0:1], scalar2=0.0, op0=ALU.mult, op1=ALU.add
                )
            st[("n", n)] = attn

        def stage_t(n):
            attn = st[("n", n)]
            xt = ps_t.tile([P, S // 2], F32, name="xt")
            words = attn[:].bitcast(F32)
            for b in range(NT // 2):
                nc.tensor.transpose(xt[:, b * P : (b + 1) * P], words[:, b * P : (b + 1) * P], ident_w[:])
            st[("t", n)] = xt

        def stage_g(n):
            xt = st[("t", n)]
            grp = work.tile([P, S], BF16, name="grp", align_bytes=64)
            dst = grp[:].bitcast(F32).rearrange("p (g q u) -> p g q u", g=2, u=2)
            src = xt[:].rearrange("p (g u q) -> p g q u", g=2, u=2)
            nc.scalar.copy(out=dst, in_=src)
            st[("g", n)] = grp

        def stage_q(n):
            grp = st[("g", n)]
            codes = work.tile([P, S // 4], U32, name="codes", align_bytes=64)
            scl = work.tile([P, S // 4], U8, name="scl", align_bytes=64)
            nc.vector.quantize_mx(out=codes[:].bitcast(FP8X4), scales=scl[:], in_=grp[:])
            st[("q", n)] = (codes, scl)

        def stage_m(n):
            h, t = divmod(n, NT)
            codes, scl = st[("q", n)]
            v_codes, v_scl = st[("v", h)]
            j = t % 4
            if n == total - 1:
                o_ps = ps_s.tile([P, 512], F32, name="s_ps")
            elif j == 0:
                o_ps = ps_o.tile([P, 512], F32, name="o_ps")
            else:
                o_ps = st[("o", n - 1)]
            st[("o", n)] = o_ps
            for g in range(2):
                cols = slice(g * P, (g + 1) * P)
                nc.tensor.matmul_mx(
                    out=o_ps[:, j * P : (j + 1) * P],
                    lhsT=codes[:, cols].bitcast(FP8X4),
                    lhsT_scale=scl[:, cols],
                    rhs=v_codes[:, cols].bitcast(FP8X4),
                    rhs_scale=v_scl[:, cols],
                    start=(g == 0),
                    stop=(g == 1),
                )

        def stage_f(n):
            h, t = divmod(n, NT)
            if n == total - 1:
                first = t
            elif n == total - 2:
                first = t - 2
            elif t % 4 == 3:
                first = t - 3
            else:
                return
            cols = slice((first % 4) * D, (t % 4 + 1) * D)
            o_sb = work.tile([P, 512], F32, name="o_sb")
            nc.vector.tensor_copy(out=o_sb[:, cols], in_=st[("o", n)][:, cols])
            nc.sync.dma_start(
                out=out[0, h].rearrange("(p t) d -> p t d", t=NT)[:, first : t + 1, :],
                in_=o_sb[:, cols].rearrange("p (t d) -> p t d", d=D),
            )

        def stage_v(n):
            h, t = divmod(n, NT)
            if t == 1:
                prep_v2(h)
            if h + 1 < H and t == 1:
                prep_v1(h + 1)

        def stage_h(n):
            h, t = divmod(n, NT)
            if h + 1 < H and t % 4 == 3:
                prep_vg(h + 1, 1, 64 * (t // 4), 64 * (t // 4) + 64)

        load(0)
        load(1)
        first_head()
        steady = (("f", 9), ("t", 5), ("s", -1), ("x", 0), ("v", 0), ("e", 2), ("r", 3), ("q", 7), ("n", 3), ("h", 0), ("b", 0), ("g", 6), ("m", 8))
        drain = (("f", 9), ("e", 2), ("r", 3), ("q", 7), ("n", 3), ("t", 5), ("g", 6), ("m", 8))
        preps = (None, prep_k, prep_k2, prep_q, prep_q2, None, None, None)
        fns = dict(f=stage_f, s=stage_s, x=stage_x, v=stage_v, e=stage_e, r=stage_r, q=stage_q, n=stage_n, b=stage_b, t=stage_t,
                   g=stage_g, m=stage_m, h=stage_h)
        todo = dict(f=0, s=1, x=0, v=0, e=0, r=0, q=0, n=0, b=0, t=0, g=0, m=0, h=0)
        for k in range(total + 10):
            for name, lag in steady if k < total else drain:
                for n in range(todo[name], min(k - lag + 1, total)):
                    fns[name](n)
                    todo[name] = n + 1
            h, t = divmod(k, NT)
            if k == 0:
                first_head_rest()
            if k < total:
                if t == 0 and h + 2 < H:
                    load(h + 2)
                if h + 1 < H and preps[t] is not None:
                    preps[t](h + 1)
